import numpy as np
import ml_dtypes


def mxq(x, axis, fmt="e4m3"):
    dtype, down = {"e4m3": (ml_dtypes.float8_e4m3fn, 7), "e5m2": (ml_dtypes.float8_e5m2, 14)}[fmt]
    v = np.moveaxis(np.asarray(x, np.float32).astype(ml_dtypes.bfloat16).astype(np.float64), axis, -1)
    blocks = v.reshape(v.shape[:-1] + (-1, 32))
    amax = np.abs(blocks).max(-1, keepdims=True)
    byte = np.maximum(np.where(amax > 0, np.frexp(amax)[1] - 1 + 127, 0) - down, 1)
    scale = np.exp2(byte - 127.0)
    codes = (blocks / scale).astype(np.float32).astype(dtype).astype(np.float64)
    return np.moveaxis((codes * scale).reshape(v.shape), -1, axis)


WIDE = False


def mx_kscale(k):
    if not WIDE:
        return np.ones(k)
    levels = np.array([30, -30])
    if k % 512:
        return np.exp2(np.random.permutation(np.resize(levels, k // 32))).repeat(32)
    a = np.empty((k // 512, 16))
    for p in range(k // 512):
        a[p, :8] = np.random.permutation(np.resize(levels, 8))
        for g in range(8):
            far = levels[np.abs(levels - a[p, g]) >= 10]
            a[p, g + 8] = far[np.random.randint(len(far))]
    return np.exp2(a.ravel()).repeat(32)


BF16 = ml_dtypes.bfloat16


def bf(x):
    return np.asarray(x, np.float32).astype(BF16)


def f64(x):
    return np.asarray(x).astype(np.float64)


B, NV, NH, NT = 4096, 2048, 512, 2


def softplus(v):
    return np.logaddexp(v, 0.0)


def softmax_last(v):
    e = np.exp(v - v.max(axis=1, keepdims=True))
    return e / e.sum(axis=1, keepdims=True)


def setup_inputs():
    s = mx_kscale(NV)
    return {"input_data": bf(np.random.standard_normal((B, NV)) * s),
            "W": bf(np.random.standard_normal((NH, NV)) / np.sqrt(NV) / s[None, :]),
            "U": bf(np.random.standard_normal((NH, NT)) * 0.5),
            "h_bias": bf(np.random.standard_normal((1, NH)) * 0.5 - np.log(NH / 16.0)),
            "y_bias": bf(np.random.standard_normal((1, NT)) * 0.5)}


def reference(input_data, W, U, h_bias, y_bias):
    pf = (mxq(f64(input_data), 1, "e5m2") @ mxq(f64(W), 1, "e4m3").T) + f64(h_bias)
    sp = softplus(pf[:, :, None] + f64(U)[None, :, :])
    logits = f64(y_bias) + sp.sum(axis=1)
    return softmax_last(logits)

@@ -1,0 +1,286 @@
+from contextlib import ExitStack
+
+import concourse.mybir as mybir
+from concourse.masks import make_identity
+
+B, NV, NH, NT = 4096, 2048, 512, 2
+FLOPS = 2 * B * NV * NH
+
+F32 = mybir.dt.float32
+BF16 = mybir.dt.bfloat16
+U32 = mybir.dt.uint32
+U8 = mybir.dt.uint8
+E4M3X4 = mybir.dt.float8_e4m3fn_x4
+E5M2X4 = mybir.dt.float8_e5m2_x4
+ALU = mybir.AluOpType
+ACT = mybir.ActivationFunctionType
+
+P = 128
+SUB = 4
+GROUP = P * SUB
+K_PASS = 512
+K_HALF = NV // 2
+HALF_PASSES = K_HALF // K_PASS
+PASSES = NV // K_PASS
+GROUPS = B // GROUP
+ROWS_PER_PART = B // P
+OUT_COLS = ROWS_PER_PART * NT
+GAP_MAX = 40.0
+BATCH_ENDS = [2, 4, 6, 8]
+HEAD_PASSES = 1
+RAW_BUFS = 4
+SPLIT_BUFS = 3
+LN_SLOTS = 3
+NV_LAST = 4
+NV_FREE = 1
+NV_ADD = 0
+NV_HEAD = 0
+ADDS_PER_SLOT = 2
+SHORT_LAG = 2
+LAG_FROM = 0
+LAG_TO = 99
+LONG_LAG = 1
+UNSPLIT_AT = (2,)
+Q_FIRST_AT = (8, 9)
+NV_LN = [4, 4, 4, 0]
+ADDS = [0, 0, 0, 3]
+DIRECT = 0
+UNSPLIT = (0, 1)
+LAST_PIECES = 4
+
+
+def tile_rbm_kernel(tc, input_data, W, U, h_bias, y_bias, out):
+    nc = tc.nc
+    x_rows = input_data.rearrange("(p i) k -> p i k", i=ROWS_PER_PART)
+    w_rows = W.rearrange("(p q) k -> p q k", q=SUB)
+
+    steps = []
+    for c in range(0, PASSES, HEAD_PASSES):
+        steps.extend([(None, c, HEAD_PASSES), (0, c, HEAD_PASSES)])
+    for g in range(1, GROUPS):
+        steps.extend([(g, c, 2) for c in range(0, PASSES, 2)])
+    n_steps = len(steps)
+
+    with ExitStack() as ctx:
+        keep = ctx.enter_context(tc.tile_pool(name="keep", bufs=1))
+        raw_pool = ctx.enter_context(tc.tile_pool(name="raw", bufs=RAW_BUFS))
+        split_pool = ctx.enter_context(tc.tile_pool(name="split", bufs=SPLIT_BUFS))
+        grouped_pool = ctx.enter_context(tc.tile_pool(name="grouped", bufs=3))
+        x_pool = ctx.enter_context(tc.tile_pool(name="xq", bufs=3))
+        turn_psum = ctx.enter_context(tc.psum_pool(name="turn", bufs=4))
+        mx_psum = ctx.enter_context(tc.psum_pool(name="mx", bufs=4))
+        ctx.enter_context(tc.manual_schedule())
+
+        raws, splits, groupeds, codes, scales, accs = {}, {}, {}, {}, {}, {}
+
+        def load(s):
+            g, c0, n = steps[s]
+            ks = slice(c0 * K_PASS, (c0 + n) * K_PASS)
+            rows = w_rows[:, :, ks] if g is None else x_rows[:, g * SUB : (g + 1) * SUB, ks]
+            raw = raw_pool.tile([P, SUB, n * K_PASS], BF16, name="raw", align_bytes=64)
+            nc.sync.dma_start(out=raw[:], in_=rows)
+            raws[s] = raw
+
+        def word_pairs(s):
+            return raws[s][:].rearrange("p a k -> p (a k)").bitcast(F32).rearrange("p (n u) -> p u n", u=2)
+
+        def split_words(s):
+            split = split_pool.tile([P, 2, SUB * steps[s][2] * P], F32, name="split", align_bytes=64)
+            nc.vector.tensor_copy(out=split[:], in_=word_pairs(s))
+            splits[s] = split[:]
+
+        def turn(s, n_vector):
+            n = steps[s][2]
+            grouped = grouped_pool.tile([P, SUB * n * K_PASS], BF16, name="grouped", align_bytes=64)
+            dest = grouped[:].bitcast(F32).rearrange("p (b a r u) -> p b a r u", a=2, r=P, u=2)
+            words = splits[s] if s in splits else word_pairs(s)
+            for b in range(2 * n):
+                c, a0 = b // 2, 2 * (b % 2)
+                bank = turn_psum.tile([P, 4 * P], F32, name="bank", tag="turn")
+                for a in range(2):
+                    for u in range(2):
+                        at = ((a0 + a) * n + c) * P
+                        nc.tensor.transpose(
+                            bank[:, (a * 2 + u) * P : (a * 2 + u + 1) * P], words[:, u, at : at + P], identity[:]
+                        )
+                source = bank[:].rearrange("p (a u r) -> p a r u", a=2, u=2)
+                if b >= 2 * n - n_vector:
+                    nc.vector.tensor_copy(out=dest[:, b, :, :, :], in_=source)
+                else:
+                    nc.scalar.copy(out=dest[:, b, :, :, :], in_=source)
+            groupeds[s] = grouped
+
+        def quantise(s):
+            g, c0, n = steps[s]
+            width = n * GROUP
+            if g is None:
+                code = keep.tile([P, width], U32, name="w_codes%d" % c0, align_bytes=64)
+                scale = keep.tile([P, width], U8, name="w_scales%d" % c0, align_bytes=64)
+                view = code[:].bitcast(E4M3X4)
+            else:
+                code = x_pool.tile([P, width], U32, name="x_codes", align_bytes=64)
+                scale = x_pool.tile([P, width], U8, name="x_scales", align_bytes=64)
+                view = code[:].bitcast(E5M2X4)
+            nc.vector.quantize_mx(out=view, scales=scale[:], in_=groupeds[s][:])
+            for c in range(n):
+                cols = slice(c * GROUP, (c + 1) * GROUP)
+                codes[(g, c0 + c)] = code[:, cols]
+                scales[(g, c0 + c)] = scale[:, cols]
+
+        def multiply(s):
+            g, c0, n = steps[s]
+            for q in range(SUB):
+                if c0 == 0:
+                    accs[q] = mx_psum.tile([P, GROUP], F32, name="acc")
+                w_cols = slice(q * P, (q + 1) * P)
+                for c in range(c0, c0 + n):
+                    nc.tensor.matmul_mx(
+                        out=accs[q][:],
+                        lhsT=codes[(None, c)][:, w_cols].bitcast(E4M3X4),
+                        lhsT_scale=scales[(None, c)][:, w_cols],
+                        rhs=codes[(g, c)].bitcast(E5M2X4),
+                        rhs_scale=scales[(g, c)],
+                        start=(c == 0),
+                        stop=(c == PASSES - 1),
+                    )
+                if c0 + n == PASSES:
+                    nc.scalar.activation(
+                        out=terms[:, q, g * GROUP : (g + 1) * GROUP], in_=accs[q][:], func=ACT.Sigmoid,
+                        bias=low[:, q : q + 1],
+                    )
+
+        def take_log(q, cols):
+            nc.scalar.activation(
+                out=terms[:, q, cols], in_=terms[:, q, cols], func=ACT.Ln, scale=gain[:, q : q + 1], bias=1.0
+            )
+
+        def add_units(g, q):
+            cols = slice(g * GROUP, (g + 1) * GROUP)
+            nc.vector.scalar_tensor_tensor(
+                out=terms[:, 0, cols], in0=terms[:, q, cols], scalar=rel_sign[:, q : q + 1], in1=terms[:, 0, cols],
+                op0=ALU.mult, op1=ALU.add,
+            )
+
+        def sum_partitions(i, q, stop=False):
+            at = OUT_COLS - NT - NT * i
+            nc.tensor.matmul(
+                gaps[:], lhsT=terms[:, q, i * P : (i + 1) * P], rhs=picks[:, q, at : at + OUT_COLS], start=False, stop=stop
+            )
+
+        terms = keep.tile([P, SUB, B], F32, name="terms")
+        probs = keep.tile([P, OUT_COLS], F32, name="probs")
+        picks = keep.tile([P, SUB, 2 * OUT_COLS], F32, name="picks")
+        spread = keep.tile([P, ROWS_PER_PART, NT], F32, name="spread")
+        identity = keep.tile([P, P], F32, name="identity")
+        u_sb = keep.tile([P, SUB, NT], BF16, name="u_sb")
+        h_sb = keep.tile([P, SUB], BF16, name="h_sb")
+        y_sb = keep.tile([P, NT], BF16, name="y_sb")
+        u_max = keep.tile([P, SUB], F32, name="u_max")
+        u_min = keep.tile([P, SUB], F32, name="u_min")
+        u_low = keep.tile([P, SUB], F32, name="u_low")
+        gap = keep.tile([P, SUB], F32, name="gap")
+        low = keep.tile([P, SUB], F32, name="low")
+        sig_up = keep.tile([P, SUB], F32, name="sig_up")
+        sig_down = keep.tile([P, SUB], F32, name="sig_down")
+        inv_down = keep.tile([P, SUB], F32, name="inv_down")
+        sig_diff = keep.tile([P, SUB], F32, name="sig_diff")
+        gain = keep.tile([P, SUB], F32, name="gain")
+        first_wins = keep.tile([P, SUB], F32, name="first_wins")
+        sign = keep.tile([P, SUB], F32, name="sign")
+        rel_sign = keep.tile([P, SUB], F32, name="rel_sign")
+        y_gap = keep.tile([P, 1], F32, name="y_gap")
+
+        nc.scalar.dma_start(out=u_sb[:], in_=U.rearrange("(p q) c -> p q c", q=SUB))
+        nc.scalar.dma_start(out=h_sb[:], in_=h_bias.rearrange("o (p q) -> (o p) q", q=SUB))
+        nc.scalar.dma_start(out=y_sb[:], in_=y_bias.rearrange("o c -> (o c)").partition_broadcast(P))
+        for s in range(RAW_BUFS - 1):
+            load(s)
+        make_identity(nc, identity[:])
+        nc.gpsimd.memset(picks[:], 0.0)
+        nc.gpsimd.memset(spread[:, :, 0], 1.0 / P)
+        nc.gpsimd.memset(spread[:, :, 1], -1.0 / P)
+
+        nc.vector.tensor_tensor(out=u_max[:], in0=u_sb[:, :, 0], in1=u_sb[:, :, 1], op=ALU.max)
+        nc.vector.tensor_tensor(out=u_min[:], in0=u_sb[:, :, 0], in1=u_sb[:, :, 1], op=ALU.min)
+        nc.vector.tensor_tensor(out=first_wins[:], in0=u_sb[:, :, 0], in1=u_sb[:, :, 1], op=ALU.is_ge)
+        nc.vector.scalar_tensor_tensor(
+            out=u_low[:], in0=u_max[:], scalar=-GAP_MAX, in1=u_min[:], op0=ALU.add, op1=ALU.max
+        )
+        nc.vector.tensor_scalar(out=sign[:], in0=first_wins[:], scalar1=2.0, scalar2=-1.0, op0=ALU.mult, op1=ALU.add)
+        nc.vector.tensor_tensor(out=gap[:], in0=u_max[:], in1=u_low[:], op=ALU.subtract)
+        nc.vector.tensor_tensor(out=low[:], in0=u_low[:], in1=h_sb[:], op=ALU.add)
+        nc.vector.tensor_scalar(out=rel_sign[:], in0=sign[:], scalar1=sign[:, 0:1], scalar2=None, op0=ALU.mult)
+        nc.scalar.activation(out=sig_down[:], in_=gap[:], func=ACT.Sigmoid, scale=-1.0)
+        nc.scalar.activation(out=sig_up[:], in_=gap[:], func=ACT.Sigmoid)
+        nc.vector.tensor_copy(out=picks[:, :, OUT_COLS - NT], in_=sign[:])
+        nc.vector.tensor_scalar(out=picks[:, :, OUT_COLS - 1], in0=sign[:], scalar1=-1.0, scalar2=None, op0=ALU.mult)
+        nc.vector.tensor_tensor(out=y_gap[:], in0=y_sb[:, 0:1], in1=y_sb[:, 1:2], op=ALU.subtract)
+        if 0 not in UNSPLIT:
+            split_words(0)
+        nc.vector.reciprocal(out=inv_down[:], in_=sig_down[:])
+        nc.vector.tensor_tensor(out=sig_diff[:], in0=sig_up[:], in1=sig_down[:], op=ALU.subtract)
+        nc.vector.tensor_tensor(out=gain[:], in0=sig_diff[:], in1=inv_down[:], op=ALU.mult)
+
+        adds = []
+        since = n_steps
+        batch_start = 0
+        mx_next = 0
+        n_vector = 0
+        for s in range(n_steps + 1):
+            since += 1
+            if s + RAW_BUFS - 1 < n_steps:
+                load(s + RAW_BUFS - 1)
+            if s >= 1 and s in Q_FIRST_AT:
+                quantise(s - 1)
+            if s + 1 < n_steps and s + 1 not in UNSPLIT and since not in UNSPLIT_AT:
+                split_words(s + 1)
+            if s >= 1 and s not in Q_FIRST_AT:
+                quantise(s - 1)
+            if s < n_steps:
+                n = steps[s][2]
+                if since <= len(NV_LN):
+                    n_vector = NV_LN[since - 1]
+                elif steps[s][0] in (None, 0):
+                    n_vector = NV_HEAD
+                else:
+                    n_vector = NV_FREE
+                turn(s, n_vector)
+                for i in range(min(ADDS[min(since, len(ADDS)) - 1], len(adds))):
+                    add_units(*adds.pop(0))
+            lag = 1 if s == n_steps else (LONG_LAG if LAG_FROM <= s < LAG_TO else 1) if steps[s][2] == 2 else SHORT_LAG
+            while mx_next <= s - lag:
+                g, c0, n = steps[mx_next]
+                mx_next += 1
+                if g is None:
+                    continue
+                multiply(mx_next - 1)
+                if c0 + n == PASSES and g + 1 in BATCH_ENDS[:-1]:
+                    for q in range(SUB):
+                        take_log(q, slice(batch_start * GROUP, (g + 1) * GROUP))
+                    adds.extend([(h, q) for q in range(1, SUB) for h in range(batch_start, g + 1)])
+                    batch_start = g + 1
+                    since = 0
+
+        gaps = turn_psum.tile([P, OUT_COLS], F32, name="gaps", tag="turn")
+        nc.tensor.matmul(
+            gaps[:], lhsT=y_gap[:, 0:1].to_broadcast([P, P]), rhs=spread[:].rearrange("p i c -> p (i c)"), start=True, stop=False
+        )
+        for add in adds:
+            add_units(*add)
+        for i in range(batch_start * SUB):
+            sum_partitions(i, 0)
+        for g in range(batch_start, GROUPS):
+            direct = DIRECT if g == GROUPS - 1 else 0
+            tiles = range(g * SUB, (g + 1) * SUB)
+            for q in range(SUB):
+                take_log(q, slice(g * GROUP, (g + 1) * GROUP))
+                if 0 < q < SUB - direct:
+                    add_units(g, q)
+                if q == SUB - direct - 1:
+                    for i in tiles:
+                        sum_partitions(i, 0, stop=(q == SUB - 1 and i == ROWS_PER_PART - 1))
+                elif q >= SUB - direct:
+                    for i in tiles:
+                        sum_partitions(i, q, stop=(q == SUB - 1 and i == ROWS_PER_PART - 1))
+        nc.scalar.activation(out=probs[:], in_=gaps[:], func=ACT.Sigmoid)
+        nc.sync.dma_start(out=out.rearrange("(p i) c -> p (i c)", i=ROWS_PER_PART), in_=probs[:])

@@ -28,7 +28,7 @@ OUT_COLS = ROWS_PER_PART * NT
 GAP_MAX = 40.0
 BATCH_ENDS = [2, 4, 6, 8]
 HEAD_PASSES = 1
-RAW_BUFS = 4
+RAW_BUFS = 6
 SPLIT_BUFS = 3
 LN_SLOTS = 3
 NV_LAST = 4
@@ -42,9 +42,14 @@ LAG_TO = 99
 LONG_LAG = 1
 UNSPLIT_AT = (2,)
 Q_FIRST_AT = (8, 9)
-NV_LN = [4, 4, 4, 0]
+NV_LN = [4, 4, 3, 0]
 ADDS = [0, 0, 0, 3]
 DIRECT = 0
+LAST_IN_TURN = 1
+Y_AT = 10
+SPLITS = [1, 0, 1, 1]
+LAGS = [1, 2, 2, 1]
+Q_MID = 1
 UNSPLIT = (0, 1)
 LAST_PIECES = 4
 
@@ -131,7 +136,10 @@ def tile_rbm_kernel(tc, input_data, W, U, h_bias, y_bias, out):
             g, c0, n = steps[s]
             for q in range(SUB):
                 if c0 == 0:
-                    accs[q] = mx_psum.tile([P, GROUP], F32, name="acc")
+                    if g == GROUPS - 1 and LAST_IN_TURN:
+                        accs[q] = turn_psum.tile([P, GROUP], F32, name="acc_last", tag="turn")
+                    else:
+                        accs[q] = mx_psum.tile([P, GROUP], F32, name="acc", tag="acc")
                 w_cols = slice(q * P, (q + 1) * P)
                 for c in range(c0, c0 + n):
                     nc.tensor.matmul_mx(
@@ -192,13 +200,13 @@ def tile_rbm_kernel(tc, input_data, W, U, h_bias, y_bias, out):
 
         nc.scalar.dma_start(out=u_sb[:], in_=U.rearrange("(p q) c -> p q c", q=SUB))
         nc.scalar.dma_start(out=h_sb[:], in_=h_bias.rearrange("o (p q) -> (o p) q", q=SUB))
-        nc.scalar.dma_start(out=y_sb[:], in_=y_bias.rearrange("o c -> (o c)").partition_broadcast(P))
         for s in range(RAW_BUFS - 1):
             load(s)
         make_identity(nc, identity[:])
         nc.gpsimd.memset(picks[:], 0.0)
-        nc.gpsimd.memset(spread[:, :, 0], 1.0 / P)
-        nc.gpsimd.memset(spread[:, :, 1], -1.0 / P)
+        nc.gpsimd.memset(spread[:, :, 0], 1.0)
+        nc.gpsimd.memset(spread[:, :, 1], -1.0)
+        nc.gpsimd.memset(y_sb[:], 0.0)
 
         nc.vector.tensor_tensor(out=u_max[:], in0=u_sb[:, :, 0], in1=u_sb[:, :, 1], op=ALU.max)
         nc.vector.tensor_tensor(out=u_min[:], in0=u_sb[:, :, 0], in1=u_sb[:, :, 1], op=ALU.min)
@@ -214,7 +222,6 @@ def tile_rbm_kernel(tc, input_data, W, U, h_bias, y_bias, out):
         nc.scalar.activation(out=sig_up[:], in_=gap[:], func=ACT.Sigmoid)
         nc.vector.tensor_copy(out=picks[:, :, OUT_COLS - NT], in_=sign[:])
         nc.vector.tensor_scalar(out=picks[:, :, OUT_COLS - 1], in0=sign[:], scalar1=-1.0, scalar2=None, op0=ALU.mult)
-        nc.vector.tensor_tensor(out=y_gap[:], in0=y_sb[:, 0:1], in1=y_sb[:, 1:2], op=ALU.subtract)
         if 0 not in UNSPLIT:
             split_words(0)
         nc.vector.reciprocal(out=inv_down[:], in_=sig_down[:])
@@ -225,16 +232,26 @@ def tile_rbm_kernel(tc, input_data, W, U, h_bias, y_bias, out):
         since = n_steps
         batch_start = 0
         mx_next = 0
+        split_next = 1
         n_vector = 0
         for s in range(n_steps + 1):
             since += 1
+            if s == Y_AT:
+                nc.sync.dma_start(out=y_sb[0:1, :], in_=y_bias)
             if s + RAW_BUFS - 1 < n_steps:
                 load(s + RAW_BUFS - 1)
             if s >= 1 and s in Q_FIRST_AT:
                 quantise(s - 1)
-            if s + 1 < n_steps and s + 1 not in UNSPLIT and since not in UNSPLIT_AT:
-                split_words(s + 1)
-            if s >= 1 and s not in Q_FIRST_AT:
+            phase = min(since, len(SPLITS)) - 1
+            split_next = max(split_next, s + 1)
+            for i in range(SPLITS[phase] if since < 9 else 1):
+                if i == 1 and s >= 1 and s not in Q_FIRST_AT and Q_MID:
+                    quantise(s - 1)
+                if split_next < n_steps and split_next <= s + SPLIT_BUFS - 1:
+                    if split_next not in UNSPLIT:
+                        split_words(split_next)
+                    split_next += 1
+            if s >= 1 and (steps[s - 1][0], steps[s - 1][1]) not in codes:
                 quantise(s - 1)
             if s < n_steps:
                 n = steps[s][2]
@@ -247,9 +264,11 @@ def tile_rbm_kernel(tc, input_data, W, U, h_bias, y_bias, out):
                 turn(s, n_vector)
                 for i in range(min(ADDS[min(since, len(ADDS)) - 1], len(adds))):
                     add_units(*adds.pop(0))
-            lag = 1 if s == n_steps else (LONG_LAG if LAG_FROM <= s < LAG_TO else 1) if steps[s][2] == 2 else SHORT_LAG
+            lag = 1 if s == n_steps else (LAGS[phase] if since < 9 else 1) if steps[s][2] == 2 else SHORT_LAG
             while mx_next <= s - lag:
                 g, c0, n = steps[mx_next]
+                if g == GROUPS - 1 and LAST_IN_TURN and s < n_steps - 1:
+                    break
                 mx_next += 1
                 if g is None:
                     continue
@@ -261,7 +280,8 @@ def tile_rbm_kernel(tc, input_data, W, U, h_bias, y_bias, out):
                     batch_start = g + 1
                     since = 0
 
-        gaps = turn_psum.tile([P, OUT_COLS], F32, name="gaps", tag="turn")
+        nc.vector.tensor_tensor(out=y_gap[:], in0=y_sb[:, 0:1], in1=y_sb[:, 1:2], op=ALU.subtract)
+        gaps = mx_psum.tile([P, OUT_COLS], F32, name="gaps", tag="acc")
         nc.tensor.matmul(
             gaps[:], lhsT=y_gap[:, 0:1].to_broadcast([P, P]), rhs=spread[:].rearrange("p i c -> p (i c)"), start=True, stop=False
         )

@@ -26,10 +26,11 @@ GROUPS = B // GROUP
 ROWS_PER_PART = B // P
 OUT_COLS = ROWS_PER_PART * NT
 GAP_MAX = 40.0
+RUN = 8
 BATCH_ENDS = [2, 4, 6, 8]
 HEAD_PASSES = 1
 RAW_BUFS = 6
-SPLIT_BUFS = 3
+SPLIT_BUFS = 4
 LN_SLOTS = 3
 NV_LAST = 4
 NV_FREE = 1
@@ -37,19 +38,19 @@ NV_ADD = 0
 NV_HEAD = 0
 ADDS_PER_SLOT = 2
 SHORT_LAG = 2
-LAG_FROM = 0
+LAG_FROM = 11
 LAG_TO = 99
 LONG_LAG = 1
 UNSPLIT_AT = (2,)
 Q_FIRST_AT = (8, 9)
-NV_LN = [4, 4, 3, 0]
-ADDS = [0, 0, 0, 3]
+NV_LN = [4, 4, 2, 1]
+ADDS = [0, 0, 0, 2]
 DIRECT = 0
 LAST_IN_TURN = 1
 Y_AT = 10
-SPLITS = [1, 0, 1, 1]
-LAGS = [1, 2, 2, 1]
-Q_MID = 1
+SPLITS = [1, 1, 1, 1]
+LAGS = [2, 2, 2, 2]
+Q_MID = 0
 UNSPLIT = (0, 1)
 LAST_PIECES = 4
 
@@ -86,19 +87,20 @@ def tile_rbm_kernel(tc, input_data, W, U, h_bias, y_bias, out):
             nc.sync.dma_start(out=raw[:], in_=rows)
             raws[s] = raw
 
-        def word_pairs(s):
-            return raws[s][:].rearrange("p a k -> p (a k)").bitcast(F32).rearrange("p (n u) -> p u n", u=2)
-
         def split_words(s):
             split = split_pool.tile([P, 2, SUB * steps[s][2] * P], F32, name="split", align_bytes=64)
-            nc.vector.tensor_copy(out=split[:], in_=word_pairs(s))
+            words = raws[s][:].rearrange("p a k -> p (a k)").bitcast(F32)
+            nc.vector.tensor_copy(
+                out=split[:].rearrange("p u (n i) -> p u n i", i=RUN),
+                in_=words.rearrange("p (n u i) -> p u n i", u=2, i=RUN),
+            )
             splits[s] = split[:]
 
         def turn(s, n_vector):
             n = steps[s][2]
             grouped = grouped_pool.tile([P, SUB * n * K_PASS], BF16, name="grouped", align_bytes=64)
             dest = grouped[:].bitcast(F32).rearrange("p (b a r u) -> p b a r u", a=2, r=P, u=2)
-            words = splits[s] if s in splits else word_pairs(s)
+            words = splits[s]
             for b in range(2 * n):
                 c, a0 = b // 2, 2 * (b % 2)
                 bank = turn_psum.tile([P, 4 * P], F32, name="bank", tag="turn")
@@ -210,24 +212,28 @@ def tile_rbm_kernel(tc, input_data, W, U, h_bias, y_bias, out):
 
         nc.vector.tensor_tensor(out=u_max[:], in0=u_sb[:, :, 0], in1=u_sb[:, :, 1], op=ALU.max)
         nc.vector.tensor_tensor(out=u_min[:], in0=u_sb[:, :, 0], in1=u_sb[:, :, 1], op=ALU.min)
-        nc.vector.tensor_tensor(out=first_wins[:], in0=u_sb[:, :, 0], in1=u_sb[:, :, 1], op=ALU.is_ge)
         nc.vector.scalar_tensor_tensor(
             out=u_low[:], in0=u_max[:], scalar=-GAP_MAX, in1=u_min[:], op0=ALU.add, op1=ALU.max
         )
-        nc.vector.tensor_scalar(out=sign[:], in0=first_wins[:], scalar1=2.0, scalar2=-1.0, op0=ALU.mult, op1=ALU.add)
         nc.vector.tensor_tensor(out=gap[:], in0=u_max[:], in1=u_low[:], op=ALU.subtract)
-        nc.vector.tensor_tensor(out=low[:], in0=u_low[:], in1=h_sb[:], op=ALU.add)
-        nc.vector.tensor_scalar(out=rel_sign[:], in0=sign[:], scalar1=sign[:, 0:1], scalar2=None, op0=ALU.mult)
         nc.scalar.activation(out=sig_down[:], in_=gap[:], func=ACT.Sigmoid, scale=-1.0)
         nc.scalar.activation(out=sig_up[:], in_=gap[:], func=ACT.Sigmoid)
-        nc.vector.tensor_copy(out=picks[:, :, OUT_COLS - NT], in_=sign[:])
-        nc.vector.tensor_scalar(out=picks[:, :, OUT_COLS - 1], in0=sign[:], scalar1=-1.0, scalar2=None, op0=ALU.mult)
-        if 0 not in UNSPLIT:
-            split_words(0)
-        nc.vector.reciprocal(out=inv_down[:], in_=sig_down[:])
-        nc.vector.tensor_tensor(out=sig_diff[:], in0=sig_up[:], in1=sig_down[:], op=ALU.subtract)
-        nc.vector.tensor_tensor(out=gain[:], in0=sig_diff[:], in1=inv_down[:], op=ALU.mult)
 
+        def setup(s):
+            if s == 0:
+                nc.vector.tensor_tensor(out=first_wins[:], in0=u_sb[:, :, 0], in1=u_sb[:, :, 1], op=ALU.is_ge)
+                nc.vector.tensor_tensor(out=low[:], in0=u_low[:], in1=h_sb[:], op=ALU.add)
+                nc.vector.reciprocal(out=inv_down[:], in_=sig_down[:])
+                nc.vector.tensor_tensor(out=sig_diff[:], in0=sig_up[:], in1=sig_down[:], op=ALU.subtract)
+            if s == 1:
+                nc.vector.tensor_scalar(out=sign[:], in0=first_wins[:], scalar1=2.0, scalar2=-1.0, op0=ALU.mult, op1=ALU.add)
+                nc.vector.tensor_tensor(out=gain[:], in0=sig_diff[:], in1=inv_down[:], op=ALU.mult)
+            if s == 2:
+                nc.vector.tensor_scalar(out=rel_sign[:], in0=sign[:], scalar1=sign[:, 0:1], scalar2=None, op0=ALU.mult)
+                nc.vector.tensor_copy(out=picks[:, :, OUT_COLS - NT], in_=sign[:])
+                nc.vector.tensor_scalar(out=picks[:, :, OUT_COLS - 1], in0=sign[:], scalar1=-1.0, scalar2=None, op0=ALU.mult)
+
+        split_words(0)
         adds = []
         since = n_steps
         batch_start = 0
@@ -236,6 +242,7 @@ def tile_rbm_kernel(tc, input_data, W, U, h_bias, y_bias, out):
         n_vector = 0
         for s in range(n_steps + 1):
             since += 1
+            setup(s)
             if s == Y_AT:
                 nc.sync.dma_start(out=y_sb[0:1, :], in_=y_bias)
             if s + RAW_BUFS - 1 < n_steps:
@@ -243,13 +250,11 @@ def tile_rbm_kernel(tc, input_data, W, U, h_bias, y_bias, out):
             if s >= 1 and s in Q_FIRST_AT:
                 quantise(s - 1)
             phase = min(since, len(SPLITS)) - 1
-            split_next = max(split_next, s + 1)
-            for i in range(SPLITS[phase] if since < 9 else 1):
+            for i in range(max(SPLITS[phase] if since < 9 else 1, s + 2 - split_next)):
                 if i == 1 and s >= 1 and s not in Q_FIRST_AT and Q_MID:
                     quantise(s - 1)
                 if split_next < n_steps and split_next <= s + SPLIT_BUFS - 1:
-                    if split_next not in UNSPLIT:
-                        split_words(split_next)
+                    split_words(split_next)
                     split_next += 1
             if s >= 1 and (steps[s - 1][0], steps[s - 1][1]) not in codes:
                 quantise(s - 1)
@@ -264,7 +269,7 @@ def tile_rbm_kernel(tc, input_data, W, U, h_bias, y_bias, out):
                 turn(s, n_vector)
                 for i in range(min(ADDS[min(since, len(ADDS)) - 1], len(adds))):
                     add_units(*adds.pop(0))
-            lag = 1 if s == n_steps else (LAGS[phase] if since < 9 else 1) if steps[s][2] == 2 else SHORT_LAG
+            lag = 1 if s == n_steps else (LAGS[phase] if s >= LAG_FROM else 1) if steps[s][2] == 2 else SHORT_LAG
             while mx_next <= s - lag:
                 g, c0, n = steps[mx_next]
                 if g == GROUPS - 1 and LAST_IN_TURN and s < n_steps - 1:

@@ -16,105 +16,111 @@ ALU = mybir.AluOpType
 ACT = mybir.ActivationFunctionType
 
 P = 128
-SUB = 4
-GROUP = P * SUB
-K_PASS = 512
-K_HALF = NV // 2
-HALF_PASSES = K_HALF // K_PASS
-PASSES = NV // K_PASS
+TILES = 4
+GROUP = P * TILES
 GROUPS = B // GROUP
-ROWS_PER_PART = B // P
-OUT_COLS = ROWS_PER_PART * NT
+K_PASS = 512
+PASSES = NV // K_PASS
+HALF_BLOCK = 8
+ROW_TILES = B // P
+OUT_COLS = ROW_TILES * NT
 GAP_MAX = 40.0
-RUN = 8
-BATCH_ENDS = [2, 4, 6, 8]
-HEAD_PASSES = 1
+
+LONG_PASSES = 2
+LOG_GROUPS = 2
+VECTOR_BANKS_AFTER_LOGS = (4, 4, 2)
+VECTOR_BANKS = 1
+ADDS_PER_STEP = 2
+
 RAW_BUFS = 6
 SPLIT_BUFS = 4
-LN_SLOTS = 3
-NV_LAST = 4
-NV_FREE = 1
-NV_ADD = 0
-NV_HEAD = 0
-ADDS_PER_SLOT = 2
-SHORT_LAG = 2
-LAG_FROM = 11
-LAG_TO = 99
-LONG_LAG = 1
-UNSPLIT_AT = (2,)
-Q_FIRST_AT = (8, 9)
-NV_LN = [4, 4, 2, 1]
-ADDS = [0, 0, 0, 2]
-DIRECT = 0
-LAST_IN_TURN = 1
-Y_AT = 10
-SPLITS = [1, 1, 1, 1]
-LAGS = [2, 2, 2, 2]
-Q_MID = 0
-UNSPLIT = (0, 1)
-LAST_PIECES = 4
+GROUPED_BUFS = 3
+X_CODE_BUFS = 3
 
 
 def tile_rbm_kernel(tc, input_data, W, U, h_bias, y_bias, out):
     nc = tc.nc
-    x_rows = input_data.rearrange("(p i) k -> p i k", i=ROWS_PER_PART)
-    w_rows = W.rearrange("(p q) k -> p q k", q=SUB)
+    x_rows = input_data.rearrange("(r i) k -> r i k", i=ROW_TILES)
+    w_rows = W.rearrange("(p q) k -> p q k", q=TILES)
 
     steps = []
-    for c in range(0, PASSES, HEAD_PASSES):
-        steps.extend([(None, c, HEAD_PASSES), (0, c, HEAD_PASSES)])
+    for c in range(PASSES):
+        steps.extend([(None, c, 1), (0, c, 1)])
     for g in range(1, GROUPS):
-        steps.extend([(g, c, 2) for c in range(0, PASSES, 2)])
+        steps.extend([(g, c, LONG_PASSES) for c in range(0, PASSES, LONG_PASSES)])
     n_steps = len(steps)
 
     with ExitStack() as ctx:
         keep = ctx.enter_context(tc.tile_pool(name="keep", bufs=1))
         raw_pool = ctx.enter_context(tc.tile_pool(name="raw", bufs=RAW_BUFS))
         split_pool = ctx.enter_context(tc.tile_pool(name="split", bufs=SPLIT_BUFS))
-        grouped_pool = ctx.enter_context(tc.tile_pool(name="grouped", bufs=3))
-        x_pool = ctx.enter_context(tc.tile_pool(name="xq", bufs=3))
+        grouped_pool = ctx.enter_context(tc.tile_pool(name="grouped", bufs=GROUPED_BUFS))
+        x_pool = ctx.enter_context(tc.tile_pool(name="xq", bufs=X_CODE_BUFS))
         turn_psum = ctx.enter_context(tc.psum_pool(name="turn", bufs=4))
         mx_psum = ctx.enter_context(tc.psum_pool(name="mx", bufs=4))
         ctx.enter_context(tc.manual_schedule())
+
+        terms = keep.tile([P, TILES, B], F32, name="terms")
+        probs = keep.tile([P, OUT_COLS], F32, name="probs")
+        picks = keep.tile([P, 2 * OUT_COLS - NT], F32, name="picks")
+        plus_minus = keep.tile([P, ROW_TILES, NT], F32, name="plus_minus")
+        identity = keep.tile([P, P], F32, name="identity")
+        u_sb = keep.tile([P, TILES, NT], BF16, name="u_sb")
+        h_sb = keep.tile([P, TILES], BF16, name="h_sb")
+        y_sb = keep.tile([P, NT], BF16, name="y_sb")
+        u_max = keep.tile([P, TILES], F32, name="u_max")
+        u_min = keep.tile([P, TILES], F32, name="u_min")
+        u_diff = keep.tile([P, TILES], F32, name="u_diff")
+        gap = keep.tile([P, TILES], F32, name="gap")
+        u_low = keep.tile([P, TILES], F32, name="u_low")
+        low_bias = keep.tile([P, TILES], F32, name="low_bias")
+        sig_up = keep.tile([P, TILES], F32, name="sig_up")
+        sig_down = keep.tile([P, TILES], F32, name="sig_down")
+        inv_down = keep.tile([P, TILES], F32, name="inv_down")
+        sig_diff = keep.tile([P, TILES], F32, name="sig_diff")
+        gain = keep.tile([P, TILES], F32, name="gain")
+        first_wins = keep.tile([P, TILES], F32, name="first_wins")
+        sign = keep.tile([P, TILES], F32, name="sign")
+        rel_sign = keep.tile([P, TILES - 1], F32, name="rel_sign")
+        y_gap = keep.tile([P, 1], F32, name="y_gap")
 
         raws, splits, groupeds, codes, scales, accs = {}, {}, {}, {}, {}, {}
 
         def load(s):
             g, c0, n = steps[s]
             ks = slice(c0 * K_PASS, (c0 + n) * K_PASS)
-            rows = w_rows[:, :, ks] if g is None else x_rows[:, g * SUB : (g + 1) * SUB, ks]
-            raw = raw_pool.tile([P, SUB, n * K_PASS], BF16, name="raw", align_bytes=64)
+            rows = w_rows[:, :, ks] if g is None else x_rows[:, g * TILES : (g + 1) * TILES, ks]
+            raw = raw_pool.tile([P, TILES, n * K_PASS], BF16, name="raw", align_bytes=64)
             nc.sync.dma_start(out=raw[:], in_=rows)
             raws[s] = raw
 
         def split_words(s):
-            split = split_pool.tile([P, 2, SUB * steps[s][2] * P], F32, name="split", align_bytes=64)
+            split = split_pool.tile([P, 2, TILES * steps[s][2] * P], F32, name="split", align_bytes=64)
             words = raws[s][:].rearrange("p a k -> p (a k)").bitcast(F32)
             nc.vector.tensor_copy(
-                out=split[:].rearrange("p u (n i) -> p u n i", i=RUN),
-                in_=words.rearrange("p (n u i) -> p u n i", u=2, i=RUN),
+                out=split[:].rearrange("p u (b j) -> p u b j", j=HALF_BLOCK),
+                in_=words.rearrange("p (b u j) -> p u b j", u=2, j=HALF_BLOCK),
             )
-            splits[s] = split[:]
+            splits[s] = split
 
-        def turn(s, n_vector):
+        def transpose(s, vector_banks):
             n = steps[s][2]
-            grouped = grouped_pool.tile([P, SUB * n * K_PASS], BF16, name="grouped", align_bytes=64)
-            dest = grouped[:].bitcast(F32).rearrange("p (b a r u) -> p b a r u", a=2, r=P, u=2)
-            words = splits[s]
-            for b in range(2 * n):
-                c, a0 = b // 2, 2 * (b % 2)
+            grouped = grouped_pool.tile([P, TILES * n * K_PASS], BF16, name="grouped", align_bytes=64)
+            dest = grouped[:].bitcast(F32).rearrange("p (m a r u) -> p m a r u", a=2, r=P, u=2)
+            for m in range(2 * n):
+                c, a0 = m // 2, 2 * (m % 2)
                 bank = turn_psum.tile([P, 4 * P], F32, name="bank", tag="turn")
                 for a in range(2):
                     for u in range(2):
                         at = ((a0 + a) * n + c) * P
                         nc.tensor.transpose(
-                            bank[:, (a * 2 + u) * P : (a * 2 + u + 1) * P], words[:, u, at : at + P], identity[:]
+                            bank[:, (a * 2 + u) * P : (a * 2 + u + 1) * P], splits[s][:, u, at : at + P], identity[:]
                         )
                 source = bank[:].rearrange("p (a u r) -> p a r u", a=2, u=2)
-                if b >= 2 * n - n_vector:
-                    nc.vector.tensor_copy(out=dest[:, b, :, :, :], in_=source)
+                if m >= 2 * n - vector_banks:
+                    nc.vector.tensor_copy(out=dest[:, m, :, :, :], in_=source)
                 else:
-                    nc.scalar.copy(out=dest[:, b, :, :, :], in_=source)
+                    nc.scalar.copy(out=dest[:, m, :, :, :], in_=source)
             groupeds[s] = grouped
 
         def quantise(s):
@@ -136,18 +142,17 @@ def tile_rbm_kernel(tc, input_data, W, U, h_bias, y_bias, out):
 
         def multiply(s):
             g, c0, n = steps[s]
-            for q in range(SUB):
-                if c0 == 0:
-                    if g == GROUPS - 1 and LAST_IN_TURN:
-                        accs[q] = turn_psum.tile([P, GROUP], F32, name="acc_last", tag="turn")
-                    else:
-                        accs[q] = mx_psum.tile([P, GROUP], F32, name="acc", tag="acc")
-                w_cols = slice(q * P, (q + 1) * P)
+            for q in range(TILES):
+                if c0 == 0 and g == GROUPS - 1:
+                    accs[q] = turn_psum.tile([P, GROUP], F32, name="last_acc", tag="turn")
+                elif c0 == 0:
+                    accs[q] = mx_psum.tile([P, GROUP], F32, name="acc", tag="acc")
+                units = slice(q * P, (q + 1) * P)
                 for c in range(c0, c0 + n):
                     nc.tensor.matmul_mx(
                         out=accs[q][:],
-                        lhsT=codes[(None, c)][:, w_cols].bitcast(E4M3X4),
-                        lhsT_scale=scales[(None, c)][:, w_cols],
+                        lhsT=codes[(None, c)][:, units].bitcast(E4M3X4),
+                        lhsT_scale=scales[(None, c)][:, units],
                         rhs=codes[(g, c)].bitcast(E5M2X4),
                         rhs_scale=scales[(g, c)],
                         start=(c == 0),
@@ -155,157 +160,142 @@ def tile_rbm_kernel(tc, input_data, W, U, h_bias, y_bias, out):
                     )
                 if c0 + n == PASSES:
                     nc.scalar.activation(
-                        out=terms[:, q, g * GROUP : (g + 1) * GROUP], in_=accs[q][:], func=ACT.Sigmoid,
-                        bias=low[:, q : q + 1],
+                        out=terms[:, q, g * GROUP : (g + 1) * GROUP],
+                        in_=accs[q][:],
+                        func=ACT.Sigmoid,
+                        bias=low_bias[:, q : q + 1],
                     )
 
-        def take_log(q, cols):
-            nc.scalar.activation(
-                out=terms[:, q, cols], in_=terms[:, q, cols], func=ACT.Ln, scale=gain[:, q : q + 1], bias=1.0
-            )
+        def take_log(q, g0, g1):
+            part = terms[:, q, g0 * GROUP : g1 * GROUP]
+            nc.scalar.activation(out=part, in_=part, func=ACT.Ln, scale=gain[:, q : q + 1], bias=1.0)
 
-        def add_units(g, q):
+        def add_unit_tile(g, q):
             cols = slice(g * GROUP, (g + 1) * GROUP)
             nc.vector.scalar_tensor_tensor(
-                out=terms[:, 0, cols], in0=terms[:, q, cols], scalar=rel_sign[:, q : q + 1], in1=terms[:, 0, cols],
-                op0=ALU.mult, op1=ALU.add,
+                out=terms[:, 0, cols],
+                in0=terms[:, q, cols],
+                scalar=rel_sign[:, q - 1 : q],
+                in1=terms[:, 0, cols],
+                op0=ALU.mult,
+                op1=ALU.add,
             )
 
-        def sum_partitions(i, q, stop=False):
+        def sum_partitions(i):
             at = OUT_COLS - NT - NT * i
             nc.tensor.matmul(
-                gaps[:], lhsT=terms[:, q, i * P : (i + 1) * P], rhs=picks[:, q, at : at + OUT_COLS], start=False, stop=stop
+                gaps[:],
+                lhsT=terms[:, 0, i * P : (i + 1) * P],
+                rhs=picks[:, at : at + OUT_COLS],
+                start=False,
+                stop=(i == ROW_TILES - 1),
             )
 
-        terms = keep.tile([P, SUB, B], F32, name="terms")
-        probs = keep.tile([P, OUT_COLS], F32, name="probs")
-        picks = keep.tile([P, SUB, 2 * OUT_COLS], F32, name="picks")
-        spread = keep.tile([P, ROWS_PER_PART, NT], F32, name="spread")
-        identity = keep.tile([P, P], F32, name="identity")
-        u_sb = keep.tile([P, SUB, NT], BF16, name="u_sb")
-        h_sb = keep.tile([P, SUB], BF16, name="h_sb")
-        y_sb = keep.tile([P, NT], BF16, name="y_sb")
-        u_max = keep.tile([P, SUB], F32, name="u_max")
-        u_min = keep.tile([P, SUB], F32, name="u_min")
-        u_low = keep.tile([P, SUB], F32, name="u_low")
-        gap = keep.tile([P, SUB], F32, name="gap")
-        low = keep.tile([P, SUB], F32, name="low")
-        sig_up = keep.tile([P, SUB], F32, name="sig_up")
-        sig_down = keep.tile([P, SUB], F32, name="sig_down")
-        inv_down = keep.tile([P, SUB], F32, name="inv_down")
-        sig_diff = keep.tile([P, SUB], F32, name="sig_diff")
-        gain = keep.tile([P, SUB], F32, name="gain")
-        first_wins = keep.tile([P, SUB], F32, name="first_wins")
-        sign = keep.tile([P, SUB], F32, name="sign")
-        rel_sign = keep.tile([P, SUB], F32, name="rel_sign")
-        y_gap = keep.tile([P, 1], F32, name="y_gap")
+        def make_biases():
+            nc.vector.scalar_tensor_tensor(
+                out=u_low[:], in0=u_max[:], scalar=-GAP_MAX, in1=u_min[:], op0=ALU.add, op1=ALU.max
+            )
+            nc.vector.tensor_tensor(out=first_wins[:], in0=u_sb[:, :, 0], in1=u_sb[:, :, 1], op=ALU.is_ge)
+            nc.vector.reciprocal(out=inv_down[:], in_=sig_down[:])
+            nc.vector.tensor_tensor(out=sig_diff[:], in0=sig_up[:], in1=sig_down[:], op=ALU.subtract)
+            nc.vector.tensor_tensor(out=low_bias[:], in0=u_low[:], in1=h_sb[:], op=ALU.add)
 
-        nc.scalar.dma_start(out=u_sb[:], in_=U.rearrange("(p q) c -> p q c", q=SUB))
-        nc.scalar.dma_start(out=h_sb[:], in_=h_bias.rearrange("o (p q) -> (o p) q", q=SUB))
+        def make_gains():
+            nc.vector.tensor_scalar(
+                out=sign[:], in0=first_wins[:], scalar1=2.0, scalar2=-1.0, op0=ALU.mult, op1=ALU.add
+            )
+            nc.vector.tensor_tensor(out=gain[:], in0=sig_diff[:], in1=inv_down[:], op=ALU.mult)
+
+        def make_picks():
+            nc.vector.tensor_scalar(
+                out=rel_sign[:], in0=sign[:, 1:TILES], scalar1=sign[:, 0:1], scalar2=None, op0=ALU.mult
+            )
+            nc.vector.tensor_copy(out=picks[:, OUT_COLS - 2 : OUT_COLS - 1], in_=sign[:, 0:1])
+            nc.vector.tensor_scalar(
+                out=picks[:, OUT_COLS - 1 : OUT_COLS], in0=sign[:, 0:1], scalar1=-1.0, scalar2=None, op0=ALU.mult
+            )
+
+        nc.scalar.dma_start(out=u_sb[:], in_=U.rearrange("(p q) c -> p q c", q=TILES))
+        nc.scalar.dma_start(out=h_sb[:], in_=h_bias.rearrange("o (p q) -> (o p) q", q=TILES))
         for s in range(RAW_BUFS - 1):
             load(s)
         make_identity(nc, identity[:])
         nc.gpsimd.memset(picks[:], 0.0)
-        nc.gpsimd.memset(spread[:, :, 0], 1.0)
-        nc.gpsimd.memset(spread[:, :, 1], -1.0)
+        nc.gpsimd.memset(plus_minus[:, :, 0], 1.0)
+        nc.gpsimd.memset(plus_minus[:, :, 1], -1.0)
         nc.gpsimd.memset(y_sb[:], 0.0)
 
         nc.vector.tensor_tensor(out=u_max[:], in0=u_sb[:, :, 0], in1=u_sb[:, :, 1], op=ALU.max)
         nc.vector.tensor_tensor(out=u_min[:], in0=u_sb[:, :, 0], in1=u_sb[:, :, 1], op=ALU.min)
-        nc.vector.scalar_tensor_tensor(
-            out=u_low[:], in0=u_max[:], scalar=-GAP_MAX, in1=u_min[:], op0=ALU.add, op1=ALU.max
-        )
-        nc.vector.tensor_tensor(out=gap[:], in0=u_max[:], in1=u_low[:], op=ALU.subtract)
+        nc.vector.tensor_tensor(out=u_diff[:], in0=u_max[:], in1=u_min[:], op=ALU.subtract)
+        nc.vector.tensor_scalar(out=gap[:], in0=u_diff[:], scalar1=GAP_MAX, scalar2=None, op0=ALU.min)
         nc.scalar.activation(out=sig_down[:], in_=gap[:], func=ACT.Sigmoid, scale=-1.0)
         nc.scalar.activation(out=sig_up[:], in_=gap[:], func=ACT.Sigmoid)
-
-        def setup(s):
-            if s == 0:
-                nc.vector.tensor_tensor(out=first_wins[:], in0=u_sb[:, :, 0], in1=u_sb[:, :, 1], op=ALU.is_ge)
-                nc.vector.tensor_tensor(out=low[:], in0=u_low[:], in1=h_sb[:], op=ALU.add)
-                nc.vector.reciprocal(out=inv_down[:], in_=sig_down[:])
-                nc.vector.tensor_tensor(out=sig_diff[:], in0=sig_up[:], in1=sig_down[:], op=ALU.subtract)
-            if s == 1:
-                nc.vector.tensor_scalar(out=sign[:], in0=first_wins[:], scalar1=2.0, scalar2=-1.0, op0=ALU.mult, op1=ALU.add)
-                nc.vector.tensor_tensor(out=gain[:], in0=sig_diff[:], in1=inv_down[:], op=ALU.mult)
-            if s == 2:
-                nc.vector.tensor_scalar(out=rel_sign[:], in0=sign[:], scalar1=sign[:, 0:1], scalar2=None, op0=ALU.mult)
-                nc.vector.tensor_copy(out=picks[:, :, OUT_COLS - NT], in_=sign[:])
-                nc.vector.tensor_scalar(out=picks[:, :, OUT_COLS - 1], in0=sign[:], scalar1=-1.0, scalar2=None, op0=ALU.mult)
+        constants = [make_biases, make_gains, make_picks]
 
         split_words(0)
         adds = []
-        since = n_steps
-        batch_start = 0
-        mx_next = 0
-        split_next = 1
-        n_vector = 0
+        logged = 0
+        since_logs = n_steps
+        multiplied = 0
         for s in range(n_steps + 1):
-            since += 1
-            setup(s)
-            if s == Y_AT:
-                nc.sync.dma_start(out=y_sb[0:1, :], in_=y_bias)
+            since_logs += 1
+            if s < len(constants):
+                constants[s]()
             if s + RAW_BUFS - 1 < n_steps:
                 load(s + RAW_BUFS - 1)
-            if s >= 1 and s in Q_FIRST_AT:
+            split_last = s < n_steps and steps[s][0] == 1
+            if split_last:
                 quantise(s - 1)
-            phase = min(since, len(SPLITS)) - 1
-            for i in range(max(SPLITS[phase] if since < 9 else 1, s + 2 - split_next)):
-                if i == 1 and s >= 1 and s not in Q_FIRST_AT and Q_MID:
-                    quantise(s - 1)
-                if split_next < n_steps and split_next <= s + SPLIT_BUFS - 1:
-                    split_words(split_next)
-                    split_next += 1
-            if s >= 1 and (steps[s - 1][0], steps[s - 1][1]) not in codes:
+            if s + 1 < n_steps:
+                split_words(s + 1)
+            if s >= 1 and not split_last:
                 quantise(s - 1)
-            if s < n_steps:
-                n = steps[s][2]
-                if since <= len(NV_LN):
-                    n_vector = NV_LN[since - 1]
-                elif steps[s][0] in (None, 0):
-                    n_vector = NV_HEAD
-                else:
-                    n_vector = NV_FREE
-                turn(s, n_vector)
-                for i in range(min(ADDS[min(since, len(ADDS)) - 1], len(adds))):
-                    add_units(*adds.pop(0))
-            lag = 1 if s == n_steps else (LAGS[phase] if s >= LAG_FROM else 1) if steps[s][2] == 2 else SHORT_LAG
-            while mx_next <= s - lag:
-                g, c0, n = steps[mx_next]
-                if g == GROUPS - 1 and LAST_IN_TURN and s < n_steps - 1:
-                    break
-                mx_next += 1
-                if g is None:
-                    continue
-                multiply(mx_next - 1)
-                if c0 + n == PASSES and g + 1 in BATCH_ENDS[:-1]:
-                    for q in range(SUB):
-                        take_log(q, slice(batch_start * GROUP, (g + 1) * GROUP))
-                    adds.extend([(h, q) for q in range(1, SUB) for h in range(batch_start, g + 1)])
-                    batch_start = g + 1
-                    since = 0
 
+            lag = 1
+            if s < n_steps:
+                is_long = steps[s][2] == LONG_PASSES
+                if since_logs <= len(VECTOR_BANKS_AFTER_LOGS):
+                    transpose(s, VECTOR_BANKS_AFTER_LOGS[since_logs - 1])
+                else:
+                    transpose(s, VECTOR_BANKS if is_long else 0)
+                    for g, q in adds[:ADDS_PER_STEP]:
+                        add_unit_tile(g, q)
+                    adds = adds[ADDS_PER_STEP:]
+                lag = 1 if is_long and logged == 0 else 2
+
+            while multiplied <= s - lag:
+                g, c0, n = steps[multiplied]
+                if g is not None:
+                    multiply(multiplied)
+                    if c0 + n == PASSES and g + 1 == logged + LOG_GROUPS and g + 1 < GROUPS:
+                        for q in range(TILES):
+                            take_log(q, logged, g + 1)
+                        adds.extend([(h, q) for q in range(1, TILES) for h in range(logged, g + 1)])
+                        logged = g + 1
+                        since_logs = 0
+                multiplied += 1
+
+        nc.sync.dma_start(out=y_sb[0:1, :], in_=y_bias)
         nc.vector.tensor_tensor(out=y_gap[:], in0=y_sb[:, 0:1], in1=y_sb[:, 1:2], op=ALU.subtract)
         gaps = mx_psum.tile([P, OUT_COLS], F32, name="gaps", tag="acc")
         nc.tensor.matmul(
-            gaps[:], lhsT=y_gap[:, 0:1].to_broadcast([P, P]), rhs=spread[:].rearrange("p i c -> p (i c)"), start=True, stop=False
+            gaps[:],
+            lhsT=y_gap[:, 0:1].to_broadcast([P, P]),
+            rhs=plus_minus[:].rearrange("p i c -> p (i c)"),
+            start=True,
+            stop=False,
         )
-        for add in adds:
-            add_units(*add)
-        for i in range(batch_start * SUB):
-            sum_partitions(i, 0)
-        for g in range(batch_start, GROUPS):
-            direct = DIRECT if g == GROUPS - 1 else 0
-            tiles = range(g * SUB, (g + 1) * SUB)
-            for q in range(SUB):
-                take_log(q, slice(g * GROUP, (g + 1) * GROUP))
-                if 0 < q < SUB - direct:
-                    add_units(g, q)
-                if q == SUB - direct - 1:
-                    for i in tiles:
-                        sum_partitions(i, 0, stop=(q == SUB - 1 and i == ROWS_PER_PART - 1))
-                elif q >= SUB - direct:
-                    for i in tiles:
-                        sum_partitions(i, q, stop=(q == SUB - 1 and i == ROWS_PER_PART - 1))
+        for g, q in adds:
+            add_unit_tile(g, q)
+        for i in range(logged * TILES):
+            sum_partitions(i)
+        for g in range(logged, GROUPS):
+            for q in range(TILES):
+                take_log(q, g, g + 1)
+                if q > 0:
+                    add_unit_tile(g, q)
+            for i in range(g * TILES, (g + 1) * TILES):
+                sum_partitions(i)
         nc.scalar.activation(out=probs[:], in_=gaps[:], func=ACT.Sigmoid)
-        nc.sync.dma_start(out=out.rearrange("(p i) c -> p (i c)", i=ROWS_PER_PART), in_=probs[:])
+        nc.sync.dma_start(out=out.rearrange("(r i) c -> r (i c)", i=ROW_TILES), in_=probs[:])

from contextlib import ExitStack

import concourse.mybir as mybir
from concourse.masks import make_identity

B, NV, NH, NT = 4096, 2048, 512, 2
FLOPS = 2 * B * NV * NH

F32 = mybir.dt.float32
BF16 = mybir.dt.bfloat16
U32 = mybir.dt.uint32
U8 = mybir.dt.uint8
E4M3X4 = mybir.dt.float8_e4m3fn_x4
E5M2X4 = mybir.dt.float8_e5m2_x4
ALU = mybir.AluOpType
ACT = mybir.ActivationFunctionType

P = 128
TILES = 4
GROUP = P * TILES
GROUPS = B // GROUP
K_PASS = 512
PASSES = NV // K_PASS
HALF_BLOCK = 8
ROW_TILES = B // P
OUT_COLS = ROW_TILES * NT
GAP_MAX = 40.0

LONG_PASSES = 2
LOG_GROUPS = 2
VECTOR_BANKS_AFTER_LOGS = (4, 4, 2)
VECTOR_BANKS = 1
ADDS_PER_STEP = 2

RAW_BUFS = 6
SPLIT_BUFS = 4
GROUPED_BUFS = 3
X_CODE_BUFS = 3


def tile_rbm_kernel(tc, input_data, W, U, h_bias, y_bias, out):
    nc = tc.nc
    x_rows = input_data.rearrange("(r i) k -> r i k", i=ROW_TILES)
    w_rows = W.rearrange("(p q) k -> p q k", q=TILES)

    steps = []
    for c in range(PASSES):
        steps.extend([(None, c, 1), (0, c, 1)])
    for g in range(1, GROUPS):
        steps.extend([(g, c, LONG_PASSES) for c in range(0, PASSES, LONG_PASSES)])
    n_steps = len(steps)

    with ExitStack() as ctx:
        keep = ctx.enter_context(tc.tile_pool(name="keep", bufs=1))
        raw_pool = ctx.enter_context(tc.tile_pool(name="raw", bufs=RAW_BUFS))
        split_pool = ctx.enter_context(tc.tile_pool(name="split", bufs=SPLIT_BUFS))
        grouped_pool = ctx.enter_context(tc.tile_pool(name="grouped", bufs=GROUPED_BUFS))
        x_pool = ctx.enter_context(tc.tile_pool(name="xq", bufs=X_CODE_BUFS))
        turn_psum = ctx.enter_context(tc.psum_pool(name="turn", bufs=4))
        mx_psum = ctx.enter_context(tc.psum_pool(name="mx", bufs=4))
        ctx.enter_context(tc.manual_schedule())

        terms = keep.tile([P, TILES, B], F32, name="terms")
        probs = keep.tile([P, OUT_COLS], F32, name="probs")
        picks = keep.tile([P, 2 * OUT_COLS - NT], F32, name="picks")
        plus_minus = keep.tile([P, ROW_TILES, NT], F32, name="plus_minus")
        identity = keep.tile([P, P], F32, name="identity")
        u_sb = keep.tile([P, TILES, NT], BF16, name="u_sb")
        h_sb = keep.tile([P, TILES], BF16, name="h_sb")
        y_sb = keep.tile([P, NT], BF16, name="y_sb")
        u_max = keep.tile([P, TILES], F32, name="u_max")
        u_min = keep.tile([P, TILES], F32, name="u_min")
        u_diff = keep.tile([P, TILES], F32, name="u_diff")
        gap = keep.tile([P, TILES], F32, name="gap")
        u_low = keep.tile([P, TILES], F32, name="u_low")
        low_bias = keep.tile([P, TILES], F32, name="low_bias")
        sig_up = keep.tile([P, TILES], F32, name="sig_up")
        sig_down = keep.tile([P, TILES], F32, name="sig_down")
        inv_down = keep.tile([P, TILES], F32, name="inv_down")
        sig_diff = keep.tile([P, TILES], F32, name="sig_diff")
        gain = keep.tile([P, TILES], F32, name="gain")
        first_wins = keep.tile([P, TILES], F32, name="first_wins")
        sign = keep.tile([P, TILES], F32, name="sign")
        rel_sign = keep.tile([P, TILES - 1], F32, name="rel_sign")
        y_gap = keep.tile([P, 1], F32, name="y_gap")

        raws, splits, groupeds, codes, scales, accs = {}, {}, {}, {}, {}, {}

        def load(s):
            g, c0, n = steps[s]
            ks = slice(c0 * K_PASS, (c0 + n) * K_PASS)
            rows = w_rows[:, :, ks] if g is None else x_rows[:, g * TILES : (g + 1) * TILES, ks]
            raw = raw_pool.tile([P, TILES, n * K_PASS], BF16, name="raw", align_bytes=64)
            nc.sync.dma_start(out=raw[:], in_=rows)
            raws[s] = raw

        def split_words(s):
            split = split_pool.tile([P, 2, TILES * steps[s][2] * P], F32, name="split", align_bytes=64)
            words = raws[s][:].rearrange("p a k -> p (a k)").bitcast(F32)
            nc.vector.tensor_copy(
                out=split[:].rearrange("p u (b j) -> p u b j", j=HALF_BLOCK),
                in_=words.rearrange("p (b u j) -> p u b j", u=2, j=HALF_BLOCK),
            )
            splits[s] = split

        def transpose(s, vector_banks):
            n = steps[s][2]
            grouped = grouped_pool.tile([P, TILES * n * K_PASS], BF16, name="grouped", align_bytes=64)
            dest = grouped[:].bitcast(F32).rearrange("p (m a r u) -> p m a r u", a=2, r=P, u=2)
            for m in range(2 * n):
                c, a0 = m // 2, 2 * (m % 2)
                bank = turn_psum.tile([P, 4 * P], F32, name="bank", tag="turn")
                for a in range(2):
                    for u in range(2):
                        at = ((a0 + a) * n + c) * P
                        nc.tensor.transpose(
                            bank[:, (a * 2 + u) * P : (a * 2 + u + 1) * P], splits[s][:, u, at : at + P], identity[:]
                        )
                source = bank[:].rearrange("p (a u r) -> p a r u", a=2, u=2)
                if m >= 2 * n - vector_banks:
                    nc.vector.tensor_copy(out=dest[:, m, :, :, :], in_=source)
                else:
                    nc.scalar.copy(out=dest[:, m, :, :, :], in_=source)
            groupeds[s] = grouped

        def quantise(s):
            g, c0, n = steps[s]
            width = n * GROUP
            if g is None:
                code = keep.tile([P, width], U32, name="w_codes%d" % c0, align_bytes=64)
                scale = keep.tile([P, width], U8, name="w_scales%d" % c0, align_bytes=64)
                view = code[:].bitcast(E4M3X4)
            else:
                code = x_pool.tile([P, width], U32, name="x_codes", align_bytes=64)
                scale = x_pool.tile([P, width], U8, name="x_scales", align_bytes=64)
                view = code[:].bitcast(E5M2X4)
            nc.vector.quantize_mx(out=view, scales=scale[:], in_=groupeds[s][:])
            for c in range(n):
                cols = slice(c * GROUP, (c + 1) * GROUP)
                codes[(g, c0 + c)] = code[:, cols]
                scales[(g, c0 + c)] = scale[:, cols]

        def multiply(s):
            g, c0, n = steps[s]
            for q in range(TILES):
                if c0 == 0 and g == GROUPS - 1:
                    accs[q] = turn_psum.tile([P, GROUP], F32, name="last_acc", tag="turn")
                elif c0 == 0:
                    accs[q] = mx_psum.tile([P, GROUP], F32, name="acc", tag="acc")
                units = slice(q * P, (q + 1) * P)
                for c in range(c0, c0 + n):
                    nc.tensor.matmul_mx(
                        out=accs[q][:],
                        lhsT=codes[(None, c)][:, units].bitcast(E4M3X4),
                        lhsT_scale=scales[(None, c)][:, units],
                        rhs=codes[(g, c)].bitcast(E5M2X4),
                        rhs_scale=scales[(g, c)],
                        start=(c == 0),
                        stop=(c == PASSES - 1),
                    )
                if c0 + n == PASSES:
                    nc.scalar.activation(
                        out=terms[:, q, g * GROUP : (g + 1) * GROUP],
                        in_=accs[q][:],
                        func=ACT.Sigmoid,
                        bias=low_bias[:, q : q + 1],
                    )

        def take_log(q, g0, g1):
            part = terms[:, q, g0 * GROUP : g1 * GROUP]
            nc.scalar.activation(out=part, in_=part, func=ACT.Ln, scale=gain[:, q : q + 1], bias=1.0)

        def add_unit_tile(g, q):
            cols = slice(g * GROUP, (g + 1) * GROUP)
            nc.vector.scalar_tensor_tensor(
                out=terms[:, 0, cols],
                in0=terms[:, q, cols],
                scalar=rel_sign[:, q - 1 : q],
                in1=terms[:, 0, cols],
                op0=ALU.mult,
                op1=ALU.add,
            )

        def sum_partitions(i):
            at = OUT_COLS - NT - NT * i
            nc.tensor.matmul(
                gaps[:],
                lhsT=terms[:, 0, i * P : (i + 1) * P],
                rhs=picks[:, at : at + OUT_COLS],
                start=False,
                stop=(i == ROW_TILES - 1),
            )

        def make_biases():
            nc.vector.scalar_tensor_tensor(
                out=u_low[:], in0=u_max[:], scalar=-GAP_MAX, in1=u_min[:], op0=ALU.add, op1=ALU.max
            )
            nc.vector.tensor_tensor(out=first_wins[:], in0=u_sb[:, :, 0], in1=u_sb[:, :, 1], op=ALU.is_ge)
            nc.vector.reciprocal(out=inv_down[:], in_=sig_down[:])
            nc.vector.tensor_tensor(out=sig_diff[:], in0=sig_up[:], in1=sig_down[:], op=ALU.subtract)
            nc.vector.tensor_tensor(out=low_bias[:], in0=u_low[:], in1=h_sb[:], op=ALU.add)

        def make_gains():
            nc.vector.tensor_scalar(
                out=sign[:], in0=first_wins[:], scalar1=2.0, scalar2=-1.0, op0=ALU.mult, op1=ALU.add
            )
            nc.vector.tensor_tensor(out=gain[:], in0=sig_diff[:], in1=inv_down[:], op=ALU.mult)

        def make_picks():
            nc.vector.tensor_scalar(
                out=rel_sign[:], in0=sign[:, 1:TILES], scalar1=sign[:, 0:1], scalar2=None, op0=ALU.mult
            )
            nc.vector.tensor_copy(out=picks[:, OUT_COLS - 2 : OUT_COLS - 1], in_=sign[:, 0:1])
            nc.vector.tensor_scalar(
                out=picks[:, OUT_COLS - 1 : OUT_COLS], in0=sign[:, 0:1], scalar1=-1.0, scalar2=None, op0=ALU.mult
            )

        nc.scalar.dma_start(out=u_sb[:], in_=U.rearrange("(p q) c -> p q c", q=TILES))
        nc.scalar.dma_start(out=h_sb[:], in_=h_bias.rearrange("o (p q) -> (o p) q", q=TILES))
        for s in range(RAW_BUFS - 1):
            load(s)
        make_identity(nc, identity[:])
        nc.gpsimd.memset(picks[:], 0.0)
        nc.gpsimd.memset(plus_minus[:, :, 0], 1.0)
        nc.gpsimd.memset(plus_minus[:, :, 1], -1.0)
        nc.gpsimd.memset(y_sb[:], 0.0)

        nc.vector.tensor_tensor(out=u_max[:], in0=u_sb[:, :, 0], in1=u_sb[:, :, 1], op=ALU.max)
        nc.vector.tensor_tensor(out=u_min[:], in0=u_sb[:, :, 0], in1=u_sb[:, :, 1], op=ALU.min)
        nc.vector.tensor_tensor(out=u_diff[:], in0=u_max[:], in1=u_min[:], op=ALU.subtract)
        nc.vector.tensor_scalar(out=gap[:], in0=u_diff[:], scalar1=GAP_MAX, scalar2=None, op0=ALU.min)
        nc.scalar.activation(out=sig_down[:], in_=gap[:], func=ACT.Sigmoid, scale=-1.0)
        nc.scalar.activation(out=sig_up[:], in_=gap[:], func=ACT.Sigmoid)
        constants = [make_biases, make_gains, make_picks]

        split_words(0)
        adds = []
        logged = 0
        since_logs = n_steps
        multiplied = 0
        for s in range(n_steps + 1):
            since_logs += 1
            if s < len(constants):
                constants[s]()
            if s + RAW_BUFS - 1 < n_steps:
                load(s + RAW_BUFS - 1)
            split_last = s < n_steps and steps[s][0] == 1
            if split_last:
                quantise(s - 1)
            if s + 1 < n_steps:
                split_words(s + 1)
            if s >= 1 and not split_last:
                quantise(s - 1)

            lag = 1
            if s < n_steps:
                is_long = steps[s][2] == LONG_PASSES
                if since_logs <= len(VECTOR_BANKS_AFTER_LOGS):
                    transpose(s, VECTOR_BANKS_AFTER_LOGS[since_logs - 1])
                else:
                    transpose(s, VECTOR_BANKS if is_long else 0)
                    for g, q in adds[:ADDS_PER_STEP]:
                        add_unit_tile(g, q)
                    adds = adds[ADDS_PER_STEP:]
                lag = 1 if is_long and logged == 0 else 2

            while multiplied <= s - lag:
                g, c0, n = steps[multiplied]
                if g is not None:
                    multiply(multiplied)
                    if c0 + n == PASSES and g + 1 == logged + LOG_GROUPS and g + 1 < GROUPS:
                        for q in range(TILES):
                            take_log(q, logged, g + 1)
                        adds.extend([(h, q) for q in range(1, TILES) for h in range(logged, g + 1)])
                        logged = g + 1
                        since_logs = 0
                multiplied += 1

        nc.sync.dma_start(out=y_sb[0:1, :], in_=y_bias)
        nc.vector.tensor_tensor(out=y_gap[:], in0=y_sb[:, 0:1], in1=y_sb[:, 1:2], op=ALU.subtract)
        gaps = mx_psum.tile([P, OUT_COLS], F32, name="gaps", tag="acc")
        nc.tensor.matmul(
            gaps[:],
            lhsT=y_gap[:, 0:1].to_broadcast([P, P]),
            rhs=plus_minus[:].rearrange("p i c -> p (i c)"),
            start=True,
            stop=False,
        )
        for g, q in adds:
            add_unit_tile(g, q)
        for i in range(logged * TILES):
            sum_partitions(i)
        for g in range(logged, GROUPS):
            for q in range(TILES):
                take_log(q, g, g + 1)
                if q > 0:
                    add_unit_tile(g, q)
            for i in range(g * TILES, (g + 1) * TILES):
                sum_partitions(i)
        nc.scalar.activation(out=probs[:], in_=gaps[:], func=ACT.Sigmoid)
        nc.sync.dma_start(out=out.rearrange("(r i) c -> r (i c)", i=ROW_TILES), in_=probs[:])
